import numpy as np
import ml_dtypes


def mxq(x, axis, fmt="e4m3"):
    dtype, down = {"e4m3": (ml_dtypes.float8_e4m3fn, 7), "e5m2": (ml_dtypes.float8_e5m2, 14)}[fmt]
    v = np.moveaxis(np.asarray(x, np.float32).astype(ml_dtypes.bfloat16).astype(np.float64), axis, -1)
    blocks = v.reshape(v.shape[:-1] + (-1, 32))
    amax = np.abs(blocks).max(-1, keepdims=True)
    byte = np.maximum(np.where(amax > 0, np.frexp(amax)[1] - 1 + 127, 0) - down, 1)
    scale = np.exp2(byte - 127.0)
    codes = (blocks / scale).astype(np.float32).astype(dtype).astype(np.float64)
    return np.moveaxis((codes * scale).reshape(v.shape), -1, axis)


WIDE = False


def mx_kscale(k):
    if not WIDE:
        return np.ones(k)
    levels = np.array([10, -10, 5, -5, 0])
    a = np.random.permutation(np.resize(levels, k // 512 * 4)).reshape(k // 512, 4)
    idx = np.arange(k)
    return np.exp2(a[idx // 512, idx % 128 // 32])


BF16 = ml_dtypes.bfloat16


def bf(x):
    return np.asarray(x, np.float32).astype(BF16)


def f64(x):
    return np.asarray(x).astype(np.float64)


E2M1 = np.array([0.0, 0.5, 1.0, 1.5, 2.0, 3.0, 4.0, 6.0, -0.0, -0.5, -1.0, -1.5, -2.0, -3.0, -4.0, -6.0])


def pack_weight(w, fmt):
    k, n = w.shape
    w = f64(bf(w)).reshape(k // 32, 32, n)
    amax = np.abs(w).max(1)
    if fmt == "e4m3":
        byte = np.frexp(amax)[1] - 1 + 127 - 7
    else:
        mant, ex = np.frexp(amax / 6.0)
        byte = np.where(mant > 0.5, ex, ex - 1) + 127
    byte = np.clip(np.where(amax > 0, byte, 1), 1, 254)
    scaled = (w * np.exp2(127.0 - byte)[:, None, :]).reshape(k, n).astype(np.float32)
    by_word = np.ascontiguousarray(scaled.reshape(k // 512, 128, 4, n).transpose(0, 1, 3, 2))
    if fmt == "e4m3":
        words = by_word.astype(ml_dtypes.float8_e4m3fn).view(np.uint8)
    else:
        c = by_word.astype(ml_dtypes.float4_e2m1fn).view(np.uint8) & 0xF
        words = c[..., 0::2] | (c[..., 1::2] << 4)
    return np.ascontiguousarray(words), np.ascontiguousarray(byte.astype(np.uint8).reshape(k // 512, 16, n))


def unpack_weight(words, scales, fmt):
    g, p, n, _ = words.shape
    if fmt == "e4m3":
        vals = np.ascontiguousarray(words).view(ml_dtypes.float8_e4m3fn).astype(np.float64)
    else:
        nib = np.empty((g, p, n, 4), np.uint8)
        nib[..., 0::2] = words & 0xF
        nib[..., 1::2] = words >> 4
        vals = E2M1[nib]
    vals = vals * np.repeat(np.exp2(scales.astype(np.float64) - 127.0), 8, axis=1)[..., None]
    return vals.transpose(0, 1, 3, 2).reshape(g * 512, n)


NS, NI, T = 4096, 2048, 129
NA = NS + NI
FMT = "e4m3"


def setup_inputs():
    s = mx_kscale(NA)
    r = s[:NS]
    A = np.random.standard_normal((NS, NS)) / np.sqrt(NA)
    B = np.random.standard_normal((NS, NI)) / np.sqrt(NA)
    x0 = np.random.standard_normal(NS) * 3.0
    V = np.random.standard_normal((T, NA))
    V[0, :NS] *= 3.0
    A_words, A_scales = pack_weight((A * r[:, None] / s[None, :NS]).T, FMT)
    B_words, B_scales = pack_weight((B * r[:, None] / s[None, NS:]).T, FMT)
    return {"A_words": A_words, "A_scales": A_scales, "B_words": B_words, "B_scales": B_scales, "x0": bf(x0 * r),
            "net_input": bf((V * s[None, :]).reshape(-1)), "T": T}


def reference(A_words, A_scales, B_words, B_scales, x0, net_input, T):
    At = unpack_weight(A_words, A_scales, FMT)
    Bt = unpack_weight(B_words, B_scales, FMT)
    ABt = np.concatenate([At, Bt], axis=0)
    n_all, n_state = ABt.shape
    V = f64(net_input).reshape(T, n_all)
    out0 = V[0, :n_state] - f64(x0)
    prop = mxq(V[:-1], 1, "e4m3") @ ABt
    out_rest = prop - V[1:, :n_state]
    return np.concatenate([out0, out_rest.reshape(-1)])

@@ -1,0 +1,148 @@
+from contextlib import ExitStack
+
+import concourse.mybir as mybir
+from concourse.masks import make_identity
+
+F32 = mybir.dt.float32
+BF16 = mybir.dt.bfloat16
+I32 = mybir.dt.int32
+U32 = mybir.dt.uint32
+U8 = mybir.dt.uint8
+FP8X4 = mybir.dt.float8_e4m3fn_x4
+
+P = 128
+PACK = 4
+K_PASS = P * PACK
+N_STATE = 4096
+N_INPUT = 2048
+N_ALL = N_STATE + N_INPUT
+STEPS = 128
+A_GROUPS = N_STATE // K_PASS
+B_GROUPS = N_INPUT // K_PASS
+GROUPS = A_GROUPS + B_GROUPS
+BANK = 512
+BANKS = N_STATE // BANK
+QUAD = 4
+QUADS = GROUPS // QUAD
+SCALE_ROWS = 4
+QUARTERS = 4
+RANGE = 1024
+RANGE_BANKS = RANGE // BANK
+RANGES = N_STATE // RANGE
+WORDS_PER_GROUP = K_PASS // 2
+FIRST_ROW_COLS = N_STATE // P
+
+FLOPS = 2 * STEPS * N_ALL * N_STATE
+
+
+def tile_constrainnet_w_kernel(tc, A_words, A_scales, B_words, B_scales, x0, net_input, T, out):
+    nc = tc.nc
+    assert T == STEPS + 1
+    steps = net_input.rearrange("(t k) -> t k", k=N_ALL)
+    later_rows = out[N_STATE:].rearrange("(t n) -> t n", n=N_STATE)
+    scale_quads = [A_scales[0:QUAD], A_scales[QUAD : 2 * QUAD], B_scales[0:QUAD]]
+
+    with ExitStack() as ctx:
+        ctx.enter_context(tc.manual_schedule())
+        keep = ctx.enter_context(tc.tile_pool(name="keep", bufs=1))
+        weights = ctx.enter_context(tc.tile_pool(name="weights", bufs=10))
+        results = ctx.enter_context(tc.tile_pool(name="results", bufs=4))
+        psum = ctx.enter_context(tc.psum_pool(name="psum", bufs=BANKS))
+
+        v_rows = keep.tile([P, N_ALL], BF16)
+        nc.sync.dma_start(out=v_rows[:], in_=steps[1 : STEPS + 1, :])
+
+        first_state = keep.tile([P, FIRST_ROW_COLS], BF16)
+        given_state = keep.tile([P, FIRST_ROW_COLS], BF16)
+        nc.scalar.dma_start(out=first_state[:], in_=net_input[0:N_STATE].rearrange("(p c) -> p c", c=FIRST_ROW_COLS))
+        nc.scalar.dma_start(out=given_state[:], in_=x0.rearrange("(p c) -> p c", c=FIRST_ROW_COLS))
+
+        nc.scalar.dma_start(out=v_rows[P - 1 : P, :], in_=steps[0:1, :])
+
+        w_scales = keep.tile([P, QUADS, N_STATE], U8, align_bytes=64)
+        for quad in range(QUADS):
+            nc.vector.memset(w_scales[:, quad, :].bitcast(I32), 0)
+            for quarter in range(QUARTERS):
+                partitions = slice(32 * quarter, 32 * quarter + QUAD * SCALE_ROWS)
+                scale_rows = slice(SCALE_ROWS * quarter, SCALE_ROWS * (quarter + 1))
+                nc.sync.dma_start(
+                    out=w_scales[partitions, quad, :].bitcast(I32),
+                    in_=scale_quads[quad][:, scale_rows, :].bitcast(I32),
+                )
+
+        identity = keep.tile([P, P], F32)
+        turned = keep.tile([P, P], F32)
+        make_identity(nc, identity[:])
+        nc.vector.tensor_copy(out=turned[:, 1:P], in_=identity[:, 0 : P - 1])
+        nc.vector.tensor_copy(out=turned[:, 0:1], in_=identity[:, P - 1 : P])
+
+        first_row = keep.tile([P, FIRST_ROW_COLS], F32)
+        nc.vector.tensor_tensor(out=first_row[:], in0=first_state[:], in1=given_state[:], op=mybir.AluOpType.subtract)
+        nc.scalar.dma_start(out=out[0:N_STATE].rearrange("(p c) -> p c", c=FIRST_ROW_COLS), in_=first_row[:])
+
+        v_words = v_rows[:].bitcast(F32)
+        banks = []
+        for pair in range(GROUPS // 2):
+            bank = psum.tile([P, 2, 2, P], F32, name="flipped%d" % pair, tag="bank")
+            for member in range(2):
+                first_word = WORDS_PER_GROUP * (2 * pair + member)
+                for u in range(2):
+                    nc.tensor.transpose(
+                        out=bank[:, member, u, :],
+                        in_=v_words[:, first_word + u : first_word + WORDS_PER_GROUP : 2],
+                        identity=turned[:],
+                    )
+            banks.append(bank)
+
+        grouped = keep.tile([P, GROUPS, STEPS, PACK], BF16, align_bytes=64)
+        grouped_words = grouped[:].bitcast(F32)
+        for pair in range(GROUPS // 2):
+            copy = nc.vector.tensor_copy if pair % 2 == 0 else nc.scalar.copy
+            copy(out=grouped_words[:, 2 * pair : 2 * pair + 2, :, :], in_=banks[pair][:].rearrange("p g u t -> p g t u"))
+
+        nc.scalar.dma_start(out=v_rows[P - 1 : P, 0:N_STATE], in_=steps[STEPS : STEPS + 1, 0:N_STATE])
+
+        v_codes = keep.tile([P, GROUPS, STEPS], U32, align_bytes=64)
+        v_scales = keep.tile([P, GROUPS, STEPS], U8, align_bytes=64)
+        for quad in range(QUADS):
+            groups = slice(QUAD * quad, QUAD * (quad + 1))
+            nc.vector.quantize_mx(
+                out=v_codes[:, groups, :].rearrange("p g t -> p (g t)").bitcast(FP8X4),
+                scales=v_scales[:, groups, :].rearrange("p g t -> p (g t)"),
+                in_=grouped[:, groups, :, :].rearrange("p g t i -> p (g t i)"),
+            )
+
+        sums = [psum.tile([P, BANK], F32, name="sums%d" % b, tag="bank") for b in range(BANKS)]
+
+        def mx_pass(g, b, moving_words):
+            quad, member = divmod(g, QUAD)
+            nc.tensor.matmul_mx(
+                out=sums[b][:],
+                lhsT=v_codes[:, g, :].bitcast(FP8X4),
+                lhsT_scale=v_scales[:, g, :],
+                rhs=moving_words.bitcast(FP8X4),
+                rhs_scale=w_scales[SCALE_ROWS * member : P, quad, BANK * b : BANK * (b + 1)],
+                start=(g == 0),
+                stop=(g == GROUPS - 1),
+            )
+
+        for g in range(A_GROUPS):
+            a_words = weights.tile([P, N_STATE], U32, tag="words", align_bytes=64)
+            nc.sync.dma_start(out=a_words[:].bitcast(I32), in_=A_words[g].rearrange("p n i -> p (n i)").bitcast(I32))
+            for b in range(BANKS):
+                mx_pass(g, b, a_words[:, BANK * b : BANK * (b + 1)])
+
+        for r in range(RANGES):
+            b_words = weights.tile([P, B_GROUPS, RANGE], U32, tag="words", align_bytes=64)
+            for g in range(B_GROUPS):
+                nc.sync.dma_start(
+                    out=b_words[:, g, :].bitcast(I32),
+                    in_=B_words[g, :, RANGE * r : RANGE * (r + 1), :].rearrange("p n i -> p (n i)").bitcast(I32),
+                )
+                for half in range(RANGE_BANKS):
+                    mx_pass(A_GROUPS + g, RANGE_BANKS * r + half, b_words[:, g, BANK * half : BANK * (half + 1)])
+            for b in range(RANGE_BANKS * r, RANGE_BANKS * (r + 1)):
+                cols = slice(BANK * b, BANK * (b + 1))
+                residual = results.tile([P, BANK], F32)
+                nc.vector.tensor_tensor(out=residual[:], in0=sums[b][:], in1=v_rows[:, cols], op=mybir.AluOpType.subtract)
+                nc.scalar.dma_start(out=later_rows[:, cols], in_=residual[:])

@@ -60,21 +60,22 @@ def tile_constrainnet_w_kernel(tc, A_words, A_scales, B_words, B_scales, x0, net
         nc.scalar.dma_start(out=v_rows[P - 1 : P, :], in_=steps[0:1, :])
 
         w_scales = keep.tile([P, QUADS, N_STATE], U8, align_bytes=64)
-        for quad in range(QUADS):
-            nc.vector.memset(w_scales[:, quad, :].bitcast(I32), 0)
-            for quarter in range(QUARTERS):
-                partitions = slice(32 * quarter, 32 * quarter + QUAD * SCALE_ROWS)
-                scale_rows = slice(SCALE_ROWS * quarter, SCALE_ROWS * (quarter + 1))
-                nc.sync.dma_start(
-                    out=w_scales[partitions, quad, :].bitcast(I32),
-                    in_=scale_quads[quad][:, scale_rows, :].bitcast(I32),
-                )
+        nc.vector.memset(w_scales[:].rearrange("p q n -> p (q n)").bitcast(I32), 0)
 
         identity = keep.tile([P, P], F32)
         turned = keep.tile([P, P], F32)
         make_identity(nc, identity[:])
         nc.vector.tensor_copy(out=turned[:, 1:P], in_=identity[:, 0 : P - 1])
         nc.vector.tensor_copy(out=turned[:, 0:1], in_=identity[:, P - 1 : P])
+
+        for quad in range(QUADS):
+            for quarter in range(QUARTERS):
+                partitions = slice(32 * quarter, 32 * quarter + QUAD * SCALE_ROWS)
+                scale_rows = slice(SCALE_ROWS * quarter, SCALE_ROWS * (quarter + 1))
+                nc.gpsimd.dma_start(
+                    out=w_scales[partitions, quad, :].bitcast(F32),
+                    in_=scale_quads[quad][:, scale_rows, :].bitcast(F32),
+                )
 
         first_row = keep.tile([P, FIRST_ROW_COLS], F32)
         nc.vector.tensor_tensor(out=first_row[:], in0=first_state[:], in1=given_state[:], op=mybir.AluOpType.subtract)

@@ -46,7 +46,7 @@ def tile_constrainnet_w_kernel(tc, A_words, A_scales, B_words, B_scales, x0, net
         ctx.enter_context(tc.manual_schedule())
         keep = ctx.enter_context(tc.tile_pool(name="keep", bufs=1))
         weights = ctx.enter_context(tc.tile_pool(name="weights", bufs=10))
-        results = ctx.enter_context(tc.tile_pool(name="results", bufs=4))
+        results = ctx.enter_context(tc.tile_pool(name="results", bufs=BANKS))
         psum = ctx.enter_context(tc.psum_pool(name="psum", bufs=BANKS))
 
         v_rows = keep.tile([P, N_ALL], BF16)
@@ -60,22 +60,21 @@ def tile_constrainnet_w_kernel(tc, A_words, A_scales, B_words, B_scales, x0, net
         nc.scalar.dma_start(out=v_rows[P - 1 : P, :], in_=steps[0:1, :])
 
         w_scales = keep.tile([P, QUADS, N_STATE], U8, align_bytes=64)
-        nc.vector.memset(w_scales[:].rearrange("p q n -> p (q n)").bitcast(I32), 0)
+        for quad in range(QUADS):
+            nc.vector.memset(w_scales[:, quad, :].bitcast(I32), 0)
+            for quarter in range(QUARTERS):
+                partitions = slice(32 * quarter, 32 * quarter + QUAD * SCALE_ROWS)
+                scale_rows = slice(SCALE_ROWS * quarter, SCALE_ROWS * (quarter + 1))
+                nc.sync.dma_start(
+                    out=w_scales[partitions, quad, :].bitcast(I32),
+                    in_=scale_quads[quad][:, scale_rows, :].bitcast(I32),
+                )
 
         identity = keep.tile([P, P], F32)
         turned = keep.tile([P, P], F32)
         make_identity(nc, identity[:])
         nc.vector.tensor_copy(out=turned[:, 1:P], in_=identity[:, 0 : P - 1])
         nc.vector.tensor_copy(out=turned[:, 0:1], in_=identity[:, P - 1 : P])
-
-        for quad in range(QUADS):
-            for quarter in range(QUARTERS):
-                partitions = slice(32 * quarter, 32 * quarter + QUAD * SCALE_ROWS)
-                scale_rows = slice(SCALE_ROWS * quarter, SCALE_ROWS * (quarter + 1))
-                nc.gpsimd.dma_start(
-                    out=w_scales[partitions, quad, :].bitcast(F32),
-                    in_=scale_quads[quad][:, scale_rows, :].bitcast(F32),
-                )
 
         first_row = keep.tile([P, FIRST_ROW_COLS], F32)
         nc.vector.tensor_tensor(out=first_row[:], in0=first_state[:], in1=given_state[:], op=mybir.AluOpType.subtract)
@@ -133,6 +132,7 @@ def tile_constrainnet_w_kernel(tc, A_words, A_scales, B_words, B_scales, x0, net
             for b in range(BANKS):
                 mx_pass(g, b, a_words[:, BANK * b : BANK * (b + 1)])
 
+        b_ranges = []
         for r in range(RANGES):
             b_words = weights.tile([P, B_GROUPS, RANGE], U32, tag="words", align_bytes=64)
             for g in range(B_GROUPS):
@@ -140,10 +140,14 @@ def tile_constrainnet_w_kernel(tc, A_words, A_scales, B_words, B_scales, x0, net
                     out=b_words[:, g, :].bitcast(I32),
                     in_=B_words[g, :, RANGE * r : RANGE * (r + 1), :].rearrange("p n i -> p (n i)").bitcast(I32),
                 )
+            b_ranges.append(b_words)
+
+        for r in range(RANGES):
+            for g in range(B_GROUPS):
                 for half in range(RANGE_BANKS):
-                    mx_pass(A_GROUPS + g, RANGE_BANKS * r + half, b_words[:, g, BANK * half : BANK * (half + 1)])
+                    mx_pass(A_GROUPS + g, RANGE_BANKS * r + half, b_ranges[r][:, g, BANK * half : BANK * (half + 1)])
             for b in range(RANGE_BANKS * r, RANGE_BANKS * (r + 1)):
                 cols = slice(BANK * b, BANK * (b + 1))
                 residual = results.tile([P, BANK], F32)
                 nc.vector.tensor_tensor(out=residual[:], in0=sums[b][:], in1=v_rows[:, cols], op=mybir.AluOpType.subtract)
-                nc.scalar.dma_start(out=later_rows[:, cols], in_=residual[:])
+                nc.sync.dma_start(out=later_rows[:, cols], in_=residual[:])

@@ -26,11 +26,10 @@ QUAD = 4
 QUADS = GROUPS // QUAD
 SCALE_ROWS = 4
 QUARTERS = 4
-RANGE = 1024
-RANGE_BANKS = RANGE // BANK
-RANGES = N_STATE // RANGE
+STRETCHES = [(0, 2048), (2048, 1024), (3072, 512), (3584, 512)]
 WORDS_PER_GROUP = K_PASS // 2
 FIRST_ROW_COLS = N_STATE // P
+FIRST_ROWS = 16
 
 FLOPS = 2 * STEPS * N_ALL * N_STATE
 
@@ -40,13 +39,17 @@ def tile_constrainnet_w_kernel(tc, A_words, A_scales, B_words, B_scales, x0, net
     assert T == STEPS + 1
     steps = net_input.rearrange("(t k) -> t k", k=N_ALL)
     later_rows = out[N_STATE:].rearrange("(t n) -> t n", n=N_STATE)
+
+    def group_words(g):
+        return A_words[g] if g < A_GROUPS else B_words[g - A_GROUPS]
+
     scale_quads = [A_scales[0:QUAD], A_scales[QUAD : 2 * QUAD], B_scales[0:QUAD]]
 
     with ExitStack() as ctx:
         ctx.enter_context(tc.manual_schedule())
         keep = ctx.enter_context(tc.tile_pool(name="keep", bufs=1))
         weights = ctx.enter_context(tc.tile_pool(name="weights", bufs=10))
-        results = ctx.enter_context(tc.tile_pool(name="results", bufs=BANKS))
+        results = ctx.enter_context(tc.tile_pool(name="results", bufs=2))
         psum = ctx.enter_context(tc.psum_pool(name="psum", bufs=BANKS))
 
         v_rows = keep.tile([P, N_ALL], BF16)
@@ -57,7 +60,11 @@ def tile_constrainnet_w_kernel(tc, A_words, A_scales, B_words, B_scales, x0, net
         nc.scalar.dma_start(out=first_state[:], in_=net_input[0:N_STATE].rearrange("(p c) -> p c", c=FIRST_ROW_COLS))
         nc.scalar.dma_start(out=given_state[:], in_=x0.rearrange("(p c) -> p c", c=FIRST_ROW_COLS))
 
-        nc.scalar.dma_start(out=v_rows[P - 1 : P, :], in_=steps[0:1, :])
+        v_first = keep.tile([P, K_PASS], BF16)
+        nc.vector.memset(v_first[:], 0.0)
+        nc.scalar.dma_start(
+            out=v_first[0:FIRST_ROWS, :], in_=net_input[0 : FIRST_ROWS * K_PASS].rearrange("(g k) -> g k", k=K_PASS)
+        )
 
         w_scales = keep.tile([P, QUADS, N_STATE], U8, align_bytes=64)
         for quad in range(QUADS):
@@ -81,6 +88,10 @@ def tile_constrainnet_w_kernel(tc, A_words, A_scales, B_words, B_scales, x0, net
         nc.scalar.dma_start(out=out[0:N_STATE].rearrange("(p c) -> p c", c=FIRST_ROW_COLS), in_=first_row[:])
 
         v_words = v_rows[:].bitcast(F32)
+        first_words = v_first[:].bitcast(F32)
+        first_bank = psum.tile([P, 2, P], F32, name="first", tag="bank")
+        for u in range(2):
+            nc.tensor.transpose(out=first_bank[:, u, :], in_=first_words[:, u:WORDS_PER_GROUP:2], identity=identity[:])
         banks = []
         for pair in range(GROUPS // 2):
             bank = psum.tile([P, 2, 2, P], F32, name="flipped%d" % pair, tag="bank")
@@ -98,9 +109,11 @@ def tile_constrainnet_w_kernel(tc, A_words, A_scales, B_words, B_scales, x0, net
         grouped_words = grouped[:].bitcast(F32)
         for pair in range(GROUPS // 2):
             copy = nc.vector.tensor_copy if pair % 2 == 0 else nc.scalar.copy
-            copy(out=grouped_words[:, 2 * pair : 2 * pair + 2, :, :], in_=banks[pair][:].rearrange("p g u t -> p g t u"))
-
-        nc.scalar.dma_start(out=v_rows[P - 1 : P, 0:N_STATE], in_=steps[STEPS : STEPS + 1, 0:N_STATE])
+            copy(
+                out=grouped_words[:, 2 * pair : 2 * pair + 2, 1:STEPS, :],
+                in_=banks[pair][:, :, :, 1:STEPS].rearrange("p g u t -> p g t u"),
+            )
+        nc.vector.tensor_copy(out=grouped_words[:, :, 0, :], in_=first_bank[:, :, 0:GROUPS].rearrange("p u g -> p g u"))
 
         v_codes = keep.tile([P, GROUPS, STEPS], U32, align_bytes=64)
         v_scales = keep.tile([P, GROUPS, STEPS], U8, align_bytes=64)
@@ -126,28 +139,28 @@ def tile_constrainnet_w_kernel(tc, A_words, A_scales, B_words, B_scales, x0, net
                 stop=(g == GROUPS - 1),
             )
 
-        for g in range(A_GROUPS):
-            a_words = weights.tile([P, N_STATE], U32, tag="words", align_bytes=64)
-            nc.sync.dma_start(out=a_words[:].bitcast(I32), in_=A_words[g].rearrange("p n i -> p (n i)").bitcast(I32))
+        for g in range(GROUPS - 1):
+            words = weights.tile([P, N_STATE], U32, tag="words", align_bytes=64)
+            nc.sync.dma_start(out=words[:].bitcast(I32), in_=group_words(g).rearrange("p n i -> p (n i)").bitcast(I32))
             for b in range(BANKS):
-                mx_pass(g, b, a_words[:, BANK * b : BANK * (b + 1)])
+                mx_pass(g, b, words[:, BANK * b : BANK * (b + 1)])
 
-        b_ranges = []
-        for r in range(RANGES):
-            b_words = weights.tile([P, B_GROUPS, RANGE], U32, tag="words", align_bytes=64)
-            for g in range(B_GROUPS):
-                nc.sync.dma_start(
-                    out=b_words[:, g, :].bitcast(I32),
-                    in_=B_words[g, :, RANGE * r : RANGE * (r + 1), :].rearrange("p n i -> p (n i)").bitcast(I32),
-                )
-            b_ranges.append(b_words)
-
-        for r in range(RANGES):
-            for g in range(B_GROUPS):
-                for half in range(RANGE_BANKS):
-                    mx_pass(A_GROUPS + g, RANGE_BANKS * r + half, b_ranges[r][:, g, BANK * half : BANK * (half + 1)])
-            for b in range(RANGE_BANKS * r, RANGE_BANKS * (r + 1)):
+        last = GROUPS - 1
+        last_words = weights.tile([P, N_STATE], U32, tag="words", align_bytes=64)
+        for first, width in STRETCHES:
+            nc.sync.dma_start(
+                out=last_words[:, first : first + width].bitcast(I32),
+                in_=group_words(last)[:, first : first + width, :].rearrange("p n i -> p (n i)").bitcast(I32),
+            )
+        for first, width in STRETCHES:
+            residual = results.tile([P, width], F32, name="residual", tag="residual%d" % width)
+            for b in range(first // BANK, (first + width) // BANK):
                 cols = slice(BANK * b, BANK * (b + 1))
-                residual = results.tile([P, BANK], F32)
-                nc.vector.tensor_tensor(out=residual[:], in0=sums[b][:], in1=v_rows[:, cols], op=mybir.AluOpType.subtract)
-                nc.sync.dma_start(out=later_rows[:, cols], in_=residual[:])
+                mx_pass(last, b, last_words[:, cols])
+                nc.vector.tensor_tensor(
+                    out=residual[:, BANK * b - first : BANK * (b + 1) - first],
+                    in0=sums[b][:],
+                    in1=v_rows[:, cols],
+                    op=mybir.AluOpType.subtract,
+                )
+            nc.sync.dma_start(out=later_rows[:, first : first + width], in_=residual[:])

@@ -26,7 +26,9 @@ QUAD = 4
 QUADS = GROUPS // QUAD
 SCALE_ROWS = 4
 QUARTERS = 4
-STRETCHES = [(0, 2048), (2048, 1024), (3072, 512), (3584, 512)]
+LATE_GROUPS = 2
+WHOLE_GROUPS = GROUPS - LATE_GROUPS
+STRETCHES = [(0, 1024), (1024, 1024), (2048, 1024), (3072, 512), (3584, 512)]
 WORDS_PER_GROUP = K_PASS // 2
 FIRST_ROW_COLS = N_STATE // P
 FIRST_ROWS = 16
@@ -49,7 +51,7 @@ def tile_constrainnet_w_kernel(tc, A_words, A_scales, B_words, B_scales, x0, net
         ctx.enter_context(tc.manual_schedule())
         keep = ctx.enter_context(tc.tile_pool(name="keep", bufs=1))
         weights = ctx.enter_context(tc.tile_pool(name="weights", bufs=10))
-        results = ctx.enter_context(tc.tile_pool(name="results", bufs=2))
+        results = ctx.enter_context(tc.tile_pool(name="results", bufs=3))
         psum = ctx.enter_context(tc.psum_pool(name="psum", bufs=BANKS))
 
         v_rows = keep.tile([P, N_ALL], BF16)
@@ -139,24 +141,28 @@ def tile_constrainnet_w_kernel(tc, A_words, A_scales, B_words, B_scales, x0, net
                 stop=(g == GROUPS - 1),
             )
 
-        for g in range(GROUPS - 1):
+        for g in range(WHOLE_GROUPS):
             words = weights.tile([P, N_STATE], U32, tag="words", align_bytes=64)
             nc.sync.dma_start(out=words[:].bitcast(I32), in_=group_words(g).rearrange("p n i -> p (n i)").bitcast(I32))
             for b in range(BANKS):
                 mx_pass(g, b, words[:, BANK * b : BANK * (b + 1)])
 
-        last = GROUPS - 1
-        last_words = weights.tile([P, N_STATE], U32, tag="words", align_bytes=64)
+        late_groups = range(WHOLE_GROUPS, GROUPS)
+        late_words = [
+            weights.tile([P, N_STATE], U32, name="late_words%d" % g, tag="words", align_bytes=64) for g in late_groups
+        ]
         for first, width in STRETCHES:
-            nc.sync.dma_start(
-                out=last_words[:, first : first + width].bitcast(I32),
-                in_=group_words(last)[:, first : first + width, :].rearrange("p n i -> p (n i)").bitcast(I32),
-            )
+            for g, words in zip(late_groups, late_words):
+                nc.sync.dma_start(
+                    out=words[:, first : first + width].bitcast(I32),
+                    in_=group_words(g)[:, first : first + width, :].rearrange("p n i -> p (n i)").bitcast(I32),
+                )
         for first, width in STRETCHES:
             residual = results.tile([P, width], F32, name="residual", tag="residual%d" % width)
             for b in range(first // BANK, (first + width) // BANK):
                 cols = slice(BANK * b, BANK * (b + 1))
-                mx_pass(last, b, last_words[:, cols])
+                for g, words in zip(late_groups, late_words):
+                    mx_pass(g, b, words[:, cols])
                 nc.vector.tensor_tensor(
                     out=residual[:, BANK * b - first : BANK * (b + 1) - first],
                     in0=sums[b][:],

@@ -68,20 +68,22 @@ def tile_constrainnet_w_kernel(tc, A_words, A_scales, B_words, B_scales, x0, net
             out=v_first[0:FIRST_ROWS, :], in_=net_input[0 : FIRST_ROWS * K_PASS].rearrange("(g k) -> g k", k=K_PASS)
         )
 
+        identity = keep.tile([P, P], F32)
+        turned = keep.tile([P, P], F32)
+        make_identity(nc, identity[:])
+
         w_scales = keep.tile([P, QUADS, N_STATE], U8, align_bytes=64)
         for quad in range(QUADS):
             nc.vector.memset(w_scales[:, quad, :].bitcast(I32), 0)
             for quarter in range(QUARTERS):
                 partitions = slice(32 * quarter, 32 * quarter + QUAD * SCALE_ROWS)
                 scale_rows = slice(SCALE_ROWS * quarter, SCALE_ROWS * (quarter + 1))
-                nc.sync.dma_start(
-                    out=w_scales[partitions, quad, :].bitcast(I32),
-                    in_=scale_quads[quad][:, scale_rows, :].bitcast(I32),
+                queue, view = (nc.sync, I32) if quarter < QUARTERS // 2 else (nc.gpsimd, F32)
+                queue.dma_start(
+                    out=w_scales[partitions, quad, :].bitcast(view),
+                    in_=scale_quads[quad][:, scale_rows, :].bitcast(view),
                 )
 
-        identity = keep.tile([P, P], F32)
-        turned = keep.tile([P, P], F32)
-        make_identity(nc, identity[:])
         nc.vector.tensor_copy(out=turned[:, 1:P], in_=identity[:, 0 : P - 1])
         nc.vector.tensor_copy(out=turned[:, 0:1], in_=identity[:, P - 1 : P])
 

@@ -28,7 +28,8 @@ SCALE_ROWS = 4
 QUARTERS = 4
 LATE_GROUPS = 2
 WHOLE_GROUPS = GROUPS - LATE_GROUPS
-STRETCHES = [(0, 1024), (1024, 1024), (2048, 1024), (3072, 512), (3584, 512)]
+STRETCHES = [(0, 2048), (2048, 1024), (3072, 1024)]
+STORES = [(0, 1024), (1024, 1024), (2048, 1024), (3072, 512), (3584, 512)]
 WORDS_PER_GROUP = K_PASS // 2
 FIRST_ROW_COLS = N_STATE // P
 FIRST_ROWS = 16
@@ -50,7 +51,7 @@ def tile_constrainnet_w_kernel(tc, A_words, A_scales, B_words, B_scales, x0, net
     with ExitStack() as ctx:
         ctx.enter_context(tc.manual_schedule())
         keep = ctx.enter_context(tc.tile_pool(name="keep", bufs=1))
-        weights = ctx.enter_context(tc.tile_pool(name="weights", bufs=10))
+        weights = ctx.enter_context(tc.tile_pool(name="weights", bufs=8))
         results = ctx.enter_context(tc.tile_pool(name="results", bufs=3))
         psum = ctx.enter_context(tc.psum_pool(name="psum", bufs=BANKS))
 
@@ -150,21 +151,18 @@ def tile_constrainnet_w_kernel(tc, A_words, A_scales, B_words, B_scales, x0, net
                 mx_pass(g, b, words[:, BANK * b : BANK * (b + 1)])
 
         late_groups = range(WHOLE_GROUPS, GROUPS)
-        late_words = [
-            weights.tile([P, N_STATE], U32, name="late_words%d" % g, tag="words", align_bytes=64) for g in late_groups
-        ]
+        late_words = keep.tile([P, LATE_GROUPS, N_STATE], U32, align_bytes=64)
+        late_source = B_words[WHOLE_GROUPS - A_GROUPS : B_GROUPS].rearrange("g p n i -> p g (n i)").bitcast(I32)
         for first, width in STRETCHES:
-            for g, words in zip(late_groups, late_words):
-                nc.sync.dma_start(
-                    out=words[:, first : first + width].bitcast(I32),
-                    in_=group_words(g)[:, first : first + width, :].rearrange("p n i -> p (n i)").bitcast(I32),
-                )
-        for first, width in STRETCHES:
+            nc.sync.dma_start(
+                out=late_words[:, :, first : first + width].bitcast(I32), in_=late_source[:, :, first : first + width]
+            )
+        for first, width in STORES:
             residual = results.tile([P, width], F32, name="residual", tag="residual%d" % width)
             for b in range(first // BANK, (first + width) // BANK):
                 cols = slice(BANK * b, BANK * (b + 1))
-                for g, words in zip(late_groups, late_words):
-                    mx_pass(g, b, words[:, cols])
+                for g in late_groups:
+                    mx_pass(g, b, late_words[:, g - WHOLE_GROUPS, cols])
                 nc.vector.tensor_tensor(
                     out=residual[:, BANK * b - first : BANK * (b + 1) - first],
                     in0=sums[b][:],

@@ -28,7 +28,7 @@ SCALE_ROWS = 4
 QUARTERS = 4
 LATE_GROUPS = 2
 WHOLE_GROUPS = GROUPS - LATE_GROUPS
-STRETCHES = [(0, 2048), (2048, 1024), (3072, 1024)]
+STRETCHES = [(first, 1024) for first in range(0, N_STATE, 1024)]
 STORES = [(0, 1024), (1024, 1024), (2048, 1024), (3072, 512), (3584, 512)]
 WORDS_PER_GROUP = K_PASS // 2
 FIRST_ROW_COLS = N_STATE // P

@@ -79,7 +79,8 @@ def tile_constrainnet_w_kernel(tc, A_words, A_scales, B_words, B_scales, x0, net
             for quarter in range(QUARTERS):
                 partitions = slice(32 * quarter, 32 * quarter + QUAD * SCALE_ROWS)
                 scale_rows = slice(SCALE_ROWS * quarter, SCALE_ROWS * (quarter + 1))
-                queue, view = (nc.sync, I32) if quarter < QUARTERS // 2 else (nc.gpsimd, F32)
+                on_gpsimd = quad < QUADS - 1 and quarter >= QUARTERS // 2
+                queue, view = (nc.gpsimd, F32) if on_gpsimd else (nc.sync, I32)
                 queue.dma_start(
                     out=w_scales[partitions, quad, :].bitcast(view),
                     in_=scale_quads[quad][:, scale_rows, :].bitcast(view),

from contextlib import ExitStack

import concourse.mybir as mybir
from concourse.masks import make_identity

F32 = mybir.dt.float32
BF16 = mybir.dt.bfloat16
I32 = mybir.dt.int32
U32 = mybir.dt.uint32
U8 = mybir.dt.uint8
FP8X4 = mybir.dt.float8_e4m3fn_x4

P = 128
PACK = 4
K_PASS = P * PACK
N_STATE = 4096
N_INPUT = 2048
N_ALL = N_STATE + N_INPUT
STEPS = 128
A_GROUPS = N_STATE // K_PASS
B_GROUPS = N_INPUT // K_PASS
GROUPS = A_GROUPS + B_GROUPS
BANK = 512
BANKS = N_STATE // BANK
QUAD = 4
QUADS = GROUPS // QUAD
SCALE_ROWS = 4
QUARTERS = 4
LATE_GROUPS = 2
WHOLE_GROUPS = GROUPS - LATE_GROUPS
STRETCHES = [(first, 1024) for first in range(0, N_STATE, 1024)]
STORES = [(0, 1024), (1024, 1024), (2048, 1024), (3072, 512), (3584, 512)]
WORDS_PER_GROUP = K_PASS // 2
FIRST_ROW_COLS = N_STATE // P
FIRST_ROWS = 16

FLOPS = 2 * STEPS * N_ALL * N_STATE


def tile_constrainnet_w_kernel(tc, A_words, A_scales, B_words, B_scales, x0, net_input, T, out):
    nc = tc.nc
    assert T == STEPS + 1
    steps = net_input.rearrange("(t k) -> t k", k=N_ALL)
    later_rows = out[N_STATE:].rearrange("(t n) -> t n", n=N_STATE)

    def group_words(g):
        return A_words[g] if g < A_GROUPS else B_words[g - A_GROUPS]

    scale_quads = [A_scales[0:QUAD], A_scales[QUAD : 2 * QUAD], B_scales[0:QUAD]]

    with ExitStack() as ctx:
        ctx.enter_context(tc.manual_schedule())
        keep = ctx.enter_context(tc.tile_pool(name="keep", bufs=1))
        weights = ctx.enter_context(tc.tile_pool(name="weights", bufs=8))
        results = ctx.enter_context(tc.tile_pool(name="results", bufs=3))
        psum = ctx.enter_context(tc.psum_pool(name="psum", bufs=BANKS))

        v_rows = keep.tile([P, N_ALL], BF16)
        nc.sync.dma_start(out=v_rows[:], in_=steps[1 : STEPS + 1, :])

        first_state = keep.tile([P, FIRST_ROW_COLS], BF16)
        given_state = keep.tile([P, FIRST_ROW_COLS], BF16)
        nc.scalar.dma_start(out=first_state[:], in_=net_input[0:N_STATE].rearrange("(p c) -> p c", c=FIRST_ROW_COLS))
        nc.scalar.dma_start(out=given_state[:], in_=x0.rearrange("(p c) -> p c", c=FIRST_ROW_COLS))

        v_first = keep.tile([P, K_PASS], BF16)
        nc.vector.memset(v_first[:], 0.0)
        nc.scalar.dma_start(
            out=v_first[0:FIRST_ROWS, :], in_=net_input[0 : FIRST_ROWS * K_PASS].rearrange("(g k) -> g k", k=K_PASS)
        )

        identity = keep.tile([P, P], F32)
        turned = keep.tile([P, P], F32)
        make_identity(nc, identity[:])

        w_scales = keep.tile([P, QUADS, N_STATE], U8, align_bytes=64)
        for quad in range(QUADS):
            nc.vector.memset(w_scales[:, quad, :].bitcast(I32), 0)
            for quarter in range(QUARTERS):
                partitions = slice(32 * quarter, 32 * quarter + QUAD * SCALE_ROWS)
                scale_rows = slice(SCALE_ROWS * quarter, SCALE_ROWS * (quarter + 1))
                on_gpsimd = quad < QUADS - 1 and quarter >= QUARTERS // 2
                queue, view = (nc.gpsimd, F32) if on_gpsimd else (nc.sync, I32)
                queue.dma_start(
                    out=w_scales[partitions, quad, :].bitcast(view),
                    in_=scale_quads[quad][:, scale_rows, :].bitcast(view),
                )

        nc.vector.tensor_copy(out=turned[:, 1:P], in_=identity[:, 0 : P - 1])
        nc.vector.tensor_copy(out=turned[:, 0:1], in_=identity[:, P - 1 : P])

        first_row = keep.tile([P, FIRST_ROW_COLS], F32)
        nc.vector.tensor_tensor(out=first_row[:], in0=first_state[:], in1=given_state[:], op=mybir.AluOpType.subtract)
        nc.scalar.dma_start(out=out[0:N_STATE].rearrange("(p c) -> p c", c=FIRST_ROW_COLS), in_=first_row[:])

        v_words = v_rows[:].bitcast(F32)
        first_words = v_first[:].bitcast(F32)
        first_bank = psum.tile([P, 2, P], F32, name="first", tag="bank")
        for u in range(2):
            nc.tensor.transpose(out=first_bank[:, u, :], in_=first_words[:, u:WORDS_PER_GROUP:2], identity=identity[:])
        banks = []
        for pair in range(GROUPS // 2):
            bank = psum.tile([P, 2, 2, P], F32, name="flipped%d" % pair, tag="bank")
            for member in range(2):
                first_word = WORDS_PER_GROUP * (2 * pair + member)
                for u in range(2):
                    nc.tensor.transpose(
                        out=bank[:, member, u, :],
                        in_=v_words[:, first_word + u : first_word + WORDS_PER_GROUP : 2],
                        identity=turned[:],
                    )
            banks.append(bank)

        grouped = keep.tile([P, GROUPS, STEPS, PACK], BF16, align_bytes=64)
        grouped_words = grouped[:].bitcast(F32)
        for pair in range(GROUPS // 2):
            copy = nc.vector.tensor_copy if pair % 2 == 0 else nc.scalar.copy
            copy(
                out=grouped_words[:, 2 * pair : 2 * pair + 2, 1:STEPS, :],
                in_=banks[pair][:, :, :, 1:STEPS].rearrange("p g u t -> p g t u"),
            )
        nc.vector.tensor_copy(out=grouped_words[:, :, 0, :], in_=first_bank[:, :, 0:GROUPS].rearrange("p u g -> p g u"))

        v_codes = keep.tile([P, GROUPS, STEPS], U32, align_bytes=64)
        v_scales = keep.tile([P, GROUPS, STEPS], U8, align_bytes=64)
        for quad in range(QUADS):
            groups = slice(QUAD * quad, QUAD * (quad + 1))
            nc.vector.quantize_mx(
                out=v_codes[:, groups, :].rearrange("p g t -> p (g t)").bitcast(FP8X4),
                scales=v_scales[:, groups, :].rearrange("p g t -> p (g t)"),
                in_=grouped[:, groups, :, :].rearrange("p g t i -> p (g t i)"),
            )

        sums = [psum.tile([P, BANK], F32, name="sums%d" % b, tag="bank") for b in range(BANKS)]

        def mx_pass(g, b, moving_words):
            quad, member = divmod(g, QUAD)
            nc.tensor.matmul_mx(
                out=sums[b][:],
                lhsT=v_codes[:, g, :].bitcast(FP8X4),
                lhsT_scale=v_scales[:, g, :],
                rhs=moving_words.bitcast(FP8X4),
                rhs_scale=w_scales[SCALE_ROWS * member : P, quad, BANK * b : BANK * (b + 1)],
                start=(g == 0),
                stop=(g == GROUPS - 1),
            )

        for g in range(WHOLE_GROUPS):
            words = weights.tile([P, N_STATE], U32, tag="words", align_bytes=64)
            nc.sync.dma_start(out=words[:].bitcast(I32), in_=group_words(g).rearrange("p n i -> p (n i)").bitcast(I32))
            for b in range(BANKS):
                mx_pass(g, b, words[:, BANK * b : BANK * (b + 1)])

        late_groups = range(WHOLE_GROUPS, GROUPS)
        late_words = keep.tile([P, LATE_GROUPS, N_STATE], U32, align_bytes=64)
        late_source = B_words[WHOLE_GROUPS - A_GROUPS : B_GROUPS].rearrange("g p n i -> p g (n i)").bitcast(I32)
        for first, width in STRETCHES:
            nc.sync.dma_start(
                out=late_words[:, :, first : first + width].bitcast(I32), in_=late_source[:, :, first : first + width]
            )
        for first, width in STORES:
            residual = results.tile([P, width], F32, name="residual", tag="residual%d" % width)
            for b in range(first // BANK, (first + width) // BANK):
                cols = slice(BANK * b, BANK * (b + 1))
                for g in late_groups:
                    mx_pass(g, b, late_words[:, g - WHOLE_GROUPS, cols])
                nc.vector.tensor_tensor(
                    out=residual[:, BANK * b - first : BANK * (b + 1) - first],
                    in0=sums[b][:],
                    in1=v_rows[:, cols],
                    op=mybir.AluOpType.subtract,
                )
            nc.sync.dma_start(out=later_rows[:, first : first + width], in_=residual[:])
